import numpy as np
import ml_dtypes


def mxq(x, axis, fmt="e4m3"):
    dtype, down = {"e4m3": (ml_dtypes.float8_e4m3fn, 7), "e5m2": (ml_dtypes.float8_e5m2, 14)}[fmt]
    v = np.moveaxis(np.asarray(x, np.float32).astype(ml_dtypes.bfloat16).astype(np.float64), axis, -1)
    blocks = v.reshape(v.shape[:-1] + (-1, 32))
    amax = np.abs(blocks).max(-1, keepdims=True)
    byte = np.maximum(np.where(amax > 0, np.frexp(amax)[1] - 1 + 127, 0) - down, 1)
    scale = np.exp2(byte - 127.0)
    codes = (blocks / scale).astype(np.float32).astype(dtype).astype(np.float64)
    return np.moveaxis((codes * scale).reshape(v.shape), -1, axis)


WIDE = False


def mx_kscale(k):
    if not WIDE:
        return np.ones(k)
    levels = np.array([10, -10, 5, -5, 0])
    if k % 512:
        return np.exp2(np.random.permutation(np.resize(levels, k // 32))).repeat(32)
    a = np.empty((k // 512, 16))
    for p in range(k // 512):
        a[p, :8] = np.random.permutation(np.resize(levels, 8))
        for g in range(8):
            far = levels[np.abs(levels - a[p, g]) >= 10]
            a[p, g + 8] = far[np.random.randint(len(far))]
    return np.exp2(a.ravel()).repeat(32)


BF16 = ml_dtypes.bfloat16


def bf(x):
    return np.asarray(x, np.float32).astype(BF16)


def f64(x):
    return np.asarray(x).astype(np.float64)


B, S, HID, NH, DH = 4, 256, 1024, 16, 64
DQ = NH * DH


def setup_inputs():
    s = mx_kscale(DQ)
    y = np.random.standard_normal((B, S, DQ)) * 0.3 * s
    h = np.ascontiguousarray(y.reshape(B, NH, S, DH).transpose(0, 2, 1, 3))
    return {"h_attn": bf(h),
            "Wo": bf(np.random.standard_normal((DQ, HID)) * 1.5 / np.sqrt(DQ) / s[:, None]),
            "bo": bf(np.random.standard_normal(HID) * 0.3)}


def reference(h_attn, Wo, bo):
    y = f64(h_attn).transpose(0, 2, 1, 3).reshape(B, -1, DQ)
    return (mxq(y, 2, "e4m3") @ mxq(f64(Wo), 0, "e4m3")) + f64(bo)

@@ -1,0 +1,203 @@
+from contextlib import ExitStack
+
+from concourse import mybir
+from concourse.masks import make_identity
+
+BF16 = mybir.dt.bfloat16
+F32 = mybir.dt.float32
+U32 = mybir.dt.uint32
+U8 = mybir.dt.uint8
+FP8X4 = mybir.dt.float8_e4m3fn_x4
+ADD = mybir.AluOpType.add
+
+P = 128
+BATCH, TOKENS, HEADS, DH = 4, 256, 16, 64
+ROW_TOKENS = 16
+THI = TOKENS // ROW_TOKENS
+K = ROW_TOKENS * DH
+N = 1024
+PACK = 4
+PASSES = K // (PACK * P)
+N_HALF = 512
+N_HALVES = N // N_HALF
+ROUNDS = 2
+ROUND_HEADS = HEADS // ROUNDS
+JL = 8
+WORDS = DH // 4
+BANK_HEADS = 2
+BANKS = ROUND_HEADS // BANK_HEADS
+TILES = BATCH
+TILE_WORDS = PASSES * P
+RUN = 4
+
+FLOPS = 2 * BATCH * TOKENS * K * N
+
+
+def tile_reasoningmultiheadattention_pb_kernel(tc, h_attn, Wo, bo, out):
+    nc = tc.nc
+    with ExitStack() as stack:
+        const = stack.enter_context(tc.tile_pool(name="const", bufs=1))
+        keep = stack.enter_context(tc.tile_pool(name="keep", bufs=1))
+        results = stack.enter_context(tc.tile_pool(name="results", bufs=8))
+        psum = stack.enter_context(tc.psum_pool(name="psum", bufs=8))
+        stack.enter_context(tc.manual_schedule())
+
+        h_view = h_attn.rearrange(
+            "b (t8 j) (r h) d -> r (b t8) j (h d)", j=JL, r=ROUNDS
+        )
+        w_view = Wo.rearrange("(g p t) n -> g p t n", g=PASSES, t=PACK)
+        out_rows = out.flatten_outer_dims()
+
+        bias_row = const.tile([P, N], BF16)
+        ones = const.tile([P, P], BF16)
+        warm = const.tile([P, 1], BF16)
+        ident = const.tile([P, P], F32)
+        perm = const.tile([P, P], F32)
+        bias = const.tile([P, N], F32)
+        x_raw = keep.tile([P, ROUNDS, JL, ROUND_HEADS * DH], BF16)
+        by_head = keep.tile([P, ROUNDS, ROUND_HEADS * JL * DH], BF16)
+        y_grouped = keep.tile([P, ROUNDS, TILES * TILE_WORDS * PACK], BF16, align_bytes=64)
+        y_codes = keep.tile([P, ROUNDS, TILES, TILE_WORDS], U32, align_bytes=64)
+        y_scales = keep.tile([P, ROUNDS, TILES, TILE_WORDS], U8, align_bytes=64)
+        w_raw = keep.tile([P, N_HALVES, PASSES, PACK, N_HALF], BF16)
+        w_grouped = keep.tile([P, N_HALVES, PASSES, N_HALF * PACK], BF16, align_bytes=64)
+        w_codes = keep.tile([P, PASSES, N], U32, align_bytes=64)
+        w_scales = keep.tile([P, PASSES, N], U8, align_bytes=64)
+
+        def half(nh):
+            return slice(nh * N_HALF, (nh + 1) * N_HALF)
+
+        def load_x(r):
+            nc.sync.dma_start(out=x_raw[:, r], in_=h_view[r])
+
+        def load_w(nh, g):
+            nc.sync.dma_start(out=w_raw[:, nh, g], in_=w_view[g][:, :, half(nh)])
+
+        nc.vector.memset(bias_row[:], 0.0)
+        nc.vector.memset(ones[:], 1.0)
+        nc.scalar.copy(out=warm[:], in_=ones[:, 0:1])
+        load_x(0)
+        nc.sync.dma_start(out=bias_row[0:1, :], in_=bo.unsqueeze(0))
+        for nh in range(N_HALVES):
+            for g in range(PASSES):
+                load_w(nh, g)
+        load_x(1)
+
+        make_identity(nc, ident[:])
+        nc.vector.tensor_copy(
+            out=perm[:].rearrange("p (b g thi) -> p b g thi", b=BATCH, g=PASSES),
+            in_=ident[:].rearrange("p (b thi g) -> p b g thi", b=BATCH, g=PASSES),
+        )
+
+        def spread_bias():
+            for nh in range(N_HALVES):
+                spread = psum.tile([P, N_HALF], F32, name="bank")
+                nc.tensor.matmul(
+                    out=spread[:], lhsT=ones[:], rhs=bias_row[:, half(nh)], start=True, stop=True
+                )
+                nc.scalar.copy(out=bias[:, half(nh)], in_=spread[:])
+
+        def regroup_w(nh, g, copy):
+            copy(
+                out=w_grouped[:, nh, g].rearrange("p (c i t) -> p c t i", i=RUN, t=PACK),
+                in_=w_raw[:, nh, g].rearrange("p t (c i) -> p c t i", i=RUN),
+            )
+
+        def quantise_w(nh, g):
+            nc.vector.quantize_mx(
+                out=w_codes[:, g, half(nh)].bitcast(FP8X4),
+                scales=w_scales[:, g, half(nh)],
+                in_=w_grouped[:, nh, g],
+            )
+
+        def sort_heads(r, q):
+            heads = slice(BANK_HEADS * q, BANK_HEADS * (q + 1))
+            for u in range(2):
+                nc.vector.tensor_copy(
+                    out=by_head[:, r].bitcast(F32).rearrange(
+                        "p (h u j w) -> p u h j w", h=ROUND_HEADS, u=2, j=JL
+                    )[:, u, heads],
+                    in_=x_raw[:, r].rearrange("p j hd -> p (j hd)").bitcast(F32).rearrange(
+                        "p (j h w u) -> p u h j w", j=JL, h=ROUND_HEADS, u=2
+                    )[:, u, heads],
+                )
+
+        def transpose_heads(r, q):
+            bank = psum.tile([P, N_HALF], F32, name="bank")
+            for hu in range(2 * BANK_HEADS):
+                first = (2 * BANK_HEADS * q + hu) * P
+                nc.tensor.transpose(
+                    bank[:].rearrange("p (bg hu thi) -> p bg hu thi", hu=2 * BANK_HEADS, thi=THI)[:, :, hu, :],
+                    by_head[:, r].bitcast(F32)[:, first : first + P],
+                    perm[:],
+                )
+            nc.scalar.copy(
+                out=y_grouped[:, r].bitcast(F32).rearrange(
+                    "p (bg h thi u) -> p bg h thi u", h=ROUND_HEADS, thi=THI, u=2
+                )[:, :, BANK_HEADS * q : BANK_HEADS * (q + 1)],
+                in_=bank[:].rearrange(
+                    "p (bg h u thi) -> p bg h thi u", h=BANK_HEADS, u=2, thi=THI
+                ),
+            )
+
+        def quantise_y(r, i):
+            nc.vector.quantize_mx(
+                out=y_codes[:, r, i].bitcast(FP8X4),
+                scales=y_scales[:, r, i],
+                in_=y_grouped[:, r, i * TILE_WORDS * PACK : (i + 1) * TILE_WORDS * PACK],
+            )
+
+        def multiply(r, nh):
+            banks = []
+            for i in range(TILES):
+                acc = psum.tile([P, N_HALF], F32, name="bank")
+                for g in range(PASSES):
+                    nc.tensor.matmul_mx(
+                        out=acc[:],
+                        lhsT=y_codes[:, r, i, g * P : (g + 1) * P].bitcast(FP8X4),
+                        lhsT_scale=y_scales[:, r, i, g * P : (g + 1) * P],
+                        rhs=w_codes[:, g, half(nh)].bitcast(FP8X4),
+                        rhs_scale=w_scales[:, g, half(nh)],
+                        start=(g == 0),
+                        stop=(g == PASSES - 1),
+                    )
+                banks.append(acc)
+            return banks
+
+        def finish(acc, r, nh, i):
+            result = results.tile([P, N_HALF], F32, name="result")
+            nc.vector.tensor_tensor(out=result[:], in0=acc[:], in1=bias[:, half(nh)], op=ADD)
+            row = i * TOKENS + r * P
+            nc.sync.dma_start(out=out_rows[row : row + P, half(nh)], in_=result[:])
+
+        spread_bias()
+        for q in range(BANKS):
+            sort_heads(0, q)
+            transpose_heads(0, q)
+        for g in range(PASSES):
+            regroup_w(0, g, nc.vector.tensor_copy)
+        for g in range(PASSES):
+            quantise_w(0, g)
+        for g in range(PASSES):
+            regroup_w(1, g, nc.scalar.copy)
+        for i in range(TILES):
+            quantise_y(0, i)
+        first_banks = multiply(0, 0)
+        for i in range(TILES // 2):
+            finish(first_banks[i], 0, 0, i)
+        quantise_w(1, 0)
+        for q in range(BANKS):
+            sort_heads(1, q)
+            transpose_heads(1, q)
+        quantise_w(1, 1)
+        for i in range(TILES // 2, TILES):
+            finish(first_banks[i], 0, 0, i)
+        second_banks = multiply(0, 1)
+        for i in range(TILES):
+            quantise_y(1, i)
+        for i in range(TILES):
+            finish(second_banks[i], 0, 1, i)
+        for nh in range(N_HALVES):
+            banks = multiply(1, nh)
+            for i in range(TILES):
+                finish(banks[i], 1, nh, i)

@@ -26,6 +26,8 @@ JL = 8
 WORDS = DH // 4
 BANK_HEADS = 2
 BANKS = ROUND_HEADS // BANK_HEADS
+CHUNKS = 2
+CHUNK = JL // CHUNKS
 TILES = BATCH
 TILE_WORDS = PASSES * P
 RUN = 4
@@ -38,7 +40,7 @@ def tile_reasoningmultiheadattention_pb_kernel(tc, h_attn, Wo, bo, out):
     with ExitStack() as stack:
         const = stack.enter_context(tc.tile_pool(name="const", bufs=1))
         keep = stack.enter_context(tc.tile_pool(name="keep", bufs=1))
-        results = stack.enter_context(tc.tile_pool(name="results", bufs=8))
+        results = stack.enter_context(tc.tile_pool(name="results", bufs=16))
         psum = stack.enter_context(tc.psum_pool(name="psum", bufs=8))
         stack.enter_context(tc.manual_schedule())
 
@@ -53,9 +55,9 @@ def tile_reasoningmultiheadattention_pb_kernel(tc, h_attn, Wo, bo, out):
         warm = const.tile([P, 1], BF16)
         ident = const.tile([P, P], F32)
         perm = const.tile([P, P], F32)
-        bias = const.tile([P, N], F32)
+        bias = const.tile([P, N], BF16)
         x_raw = keep.tile([P, ROUNDS, JL, ROUND_HEADS * DH], BF16)
-        by_head = keep.tile([P, ROUNDS, ROUND_HEADS * JL * DH], BF16)
+        by_head = keep.tile([P, ROUNDS, 2, ROUND_HEADS * P], F32)
         y_grouped = keep.tile([P, ROUNDS, TILES * TILE_WORDS * PACK], BF16, align_bytes=64)
         y_codes = keep.tile([P, ROUNDS, TILES, TILE_WORDS], U32, align_bytes=64)
         y_scales = keep.tile([P, ROUNDS, TILES, TILE_WORDS], U8, align_bytes=64)
@@ -67,22 +69,25 @@ def tile_reasoningmultiheadattention_pb_kernel(tc, h_attn, Wo, bo, out):
         def half(nh):
             return slice(nh * N_HALF, (nh + 1) * N_HALF)
 
-        def load_x(r):
-            nc.sync.dma_start(out=x_raw[:, r], in_=h_view[r])
+        def load_x(r, c):
+            tokens = slice(c * CHUNK, (c + 1) * CHUNK)
+            nc.sync.dma_start(out=x_raw[:, r, tokens], in_=h_view[r][:, tokens])
 
         def load_w(nh, g):
             nc.sync.dma_start(out=w_raw[:, nh, g], in_=w_view[g][:, :, half(nh)])
 
-        nc.vector.memset(bias_row[:], 0.0)
         nc.vector.memset(ones[:], 1.0)
+        nc.vector.memset(bias_row[:], 0.0)
         nc.scalar.copy(out=warm[:], in_=ones[:, 0:1])
-        load_x(0)
+        load_x(0, 0)
         nc.sync.dma_start(out=bias_row[0:1, :], in_=bo.unsqueeze(0))
-        for nh in range(N_HALVES):
-            for g in range(PASSES):
-                load_w(nh, g)
-        load_x(1)
-
+        load_x(0, 1)
+        load_w(0, 0)
+        load_w(0, 1)
+        load_x(1, 0)
+        load_x(1, 1)
+        load_w(1, 0)
+        load_w(1, 1)
         make_identity(nc, ident[:])
         nc.vector.tensor_copy(
             out=perm[:].rearrange("p (b g thi) -> p b g thi", b=BATCH, g=PASSES),
@@ -90,18 +95,29 @@ def tile_reasoningmultiheadattention_pb_kernel(tc, h_attn, Wo, bo, out):
         )
 
         def spread_bias():
+            spread = psum.tile([P, N], BF16, name="bank")
             for nh in range(N_HALVES):
-                spread = psum.tile([P, N_HALF], F32, name="bank")
                 nc.tensor.matmul(
-                    out=spread[:], lhsT=ones[:], rhs=bias_row[:, half(nh)], start=True, stop=True
+                    out=spread[:, half(nh)], lhsT=ones[:], rhs=bias_row[:, half(nh)], start=True, stop=True
                 )
-                nc.scalar.copy(out=bias[:, half(nh)], in_=spread[:])
+            nc.scalar.copy(out=bias[:], in_=spread[:])
 
-        def regroup_w(nh, g, copy):
+        def regroup_w(nh, g, copy, first=0, last=N_HALF):
             copy(
-                out=w_grouped[:, nh, g].rearrange("p (c i t) -> p c t i", i=RUN, t=PACK),
-                in_=w_raw[:, nh, g].rearrange("p t (c i) -> p c t i", i=RUN),
+                out=w_grouped[:, nh, g, first * PACK : last * PACK].rearrange(
+                    "p (c i t) -> p c t i", i=RUN, t=PACK
+                ),
+                in_=w_raw[:, nh, g, :, first:last].rearrange("p t (c i) -> p c t i", i=RUN),
             )
+
+        def share_w(nh, g, cut):
+            regroup_w(nh, g, nc.vector.tensor_copy, last=cut)
+            regroup_w(nh, g, nc.scalar.copy, first=cut)
+
+        def warm_up(rhs, count):
+            bank = psum.tile([P, N_HALF], F32, name="bank")
+            for k in range(count):
+                nc.tensor.matmul(out=bank[:], lhsT=ones[:], rhs=rhs, start=True, stop=True)
 
         def quantise_w(nh, g):
             nc.vector.quantize_mx(
@@ -110,28 +126,33 @@ def tile_reasoningmultiheadattention_pb_kernel(tc, h_attn, Wo, bo, out):
                 in_=w_grouped[:, nh, g],
             )
 
-        def sort_heads(r, q):
-            heads = slice(BANK_HEADS * q, BANK_HEADS * (q + 1))
-            for u in range(2):
-                nc.vector.tensor_copy(
-                    out=by_head[:, r].bitcast(F32).rearrange(
-                        "p (h u j w) -> p u h j w", h=ROUND_HEADS, u=2, j=JL
-                    )[:, u, heads],
-                    in_=x_raw[:, r].rearrange("p j hd -> p (j hd)").bitcast(F32).rearrange(
-                        "p (j h w u) -> p u h j w", j=JL, h=ROUND_HEADS, u=2
-                    )[:, u, heads],
-                )
+        def sort_heads(r, c, u, copy, first=0, last=ROUND_HEADS):
+            tokens = slice(c * CHUNK, (c + 1) * CHUNK)
+            copy(
+                out=by_head[:, r, u].rearrange("p (h j w) -> p h j w", h=ROUND_HEADS, j=JL)[
+                    :, first:last, tokens
+                ],
+                in_=x_raw[:, r].rearrange("p j hd -> p (j hd)").bitcast(F32).rearrange(
+                    "p (j h w u) -> p u h j w", j=JL, h=ROUND_HEADS, u=2
+                )[:, u, first:last, tokens],
+            )
 
         def transpose_heads(r, q):
             bank = psum.tile([P, N_HALF], F32, name="bank")
-            for hu in range(2 * BANK_HEADS):
-                first = (2 * BANK_HEADS * q + hu) * P
-                nc.tensor.transpose(
-                    bank[:].rearrange("p (bg hu thi) -> p bg hu thi", hu=2 * BANK_HEADS, thi=THI)[:, :, hu, :],
-                    by_head[:, r].bitcast(F32)[:, first : first + P],
-                    perm[:],
-                )
-            nc.scalar.copy(
+            for h in range(BANK_HEADS):
+                for u in range(2):
+                    first = (BANK_HEADS * q + h) * P
+                    nc.tensor.transpose(
+                        bank[:].rearrange(
+                            "p (bg h u thi) -> p bg h u thi", h=BANK_HEADS, u=2, thi=THI
+                        )[:, :, h, u],
+                        by_head[:, r, u, first : first + P],
+                        perm[:],
+                    )
+            return bank
+
+        def empty_heads(bank, r, q, copy):
+            copy(
                 out=y_grouped[:, r].bitcast(F32).rearrange(
                     "p (bg h thi u) -> p bg h thi u", h=ROUND_HEADS, thi=THI, u=2
                 )[:, :, BANK_HEADS * q : BANK_HEADS * (q + 1)],
@@ -147,57 +168,80 @@ def tile_reasoningmultiheadattention_pb_kernel(tc, h_attn, Wo, bo, out):
                 in_=y_grouped[:, r, i * TILE_WORDS * PACK : (i + 1) * TILE_WORDS * PACK],
             )
 
-        def multiply(r, nh):
-            banks = []
-            for i in range(TILES):
-                acc = psum.tile([P, N_HALF], F32, name="bank")
-                for g in range(PASSES):
-                    nc.tensor.matmul_mx(
-                        out=acc[:],
-                        lhsT=y_codes[:, r, i, g * P : (g + 1) * P].bitcast(FP8X4),
-                        lhsT_scale=y_scales[:, r, i, g * P : (g + 1) * P],
-                        rhs=w_codes[:, g, half(nh)].bitcast(FP8X4),
-                        rhs_scale=w_scales[:, g, half(nh)],
-                        start=(g == 0),
-                        stop=(g == PASSES - 1),
-                    )
-                banks.append(acc)
-            return banks
+        def multiply_tile(r, nh, i):
+            acc = psum.tile([P, N_HALF], F32, name="bank")
+            for g in range(PASSES):
+                nc.tensor.matmul_mx(
+                    out=acc[:],
+                    lhsT=y_codes[:, r, i, g * P : (g + 1) * P].bitcast(FP8X4),
+                    lhsT_scale=y_scales[:, r, i, g * P : (g + 1) * P],
+                    rhs=w_codes[:, g, half(nh)].bitcast(FP8X4),
+                    rhs_scale=w_scales[:, g, half(nh)],
+                    start=(g == 0),
+                    stop=(g == PASSES - 1),
+                )
+            return acc
 
-        def finish(acc, r, nh, i):
+        def multiply(r, nh):
+            return [multiply_tile(r, nh, i) for i in range(TILES)]
+
+        def finish(acc, r, nh, i, by_scalar=False):
             result = results.tile([P, N_HALF], F32, name="result")
-            nc.vector.tensor_tensor(out=result[:], in0=acc[:], in1=bias[:, half(nh)], op=ADD)
+            if by_scalar:
+                nc.scalar.copy(out=result[:], in_=acc[:])
+                nc.gpsimd.tensor_tensor(out=result[:], in0=result[:], in1=bias[:, half(nh)], op=ADD)
+            else:
+                nc.vector.tensor_tensor(out=result[:], in0=acc[:], in1=bias[:, half(nh)], op=ADD)
             row = i * TOKENS + r * P
             nc.sync.dma_start(out=out_rows[row : row + P, half(nh)], in_=result[:])
 
+        V, S = nc.vector.tensor_copy, nc.scalar.copy
+        sort_heads(0, 0, 0, V)
+        sort_heads(0, 0, 1, V)
         spread_bias()
+        sort_heads(0, 1, 0, S)
+        sort_heads(0, 1, 1, V)
+        tb = [transpose_heads(0, q) for q in range(BANKS)]
+        share_w(0, 0, 256)
         for q in range(BANKS):
-            sort_heads(0, q)
-            transpose_heads(0, q)
-        for g in range(PASSES):
-            regroup_w(0, g, nc.vector.tensor_copy)
-        for g in range(PASSES):
-            quantise_w(0, g)
-        for g in range(PASSES):
-            regroup_w(1, g, nc.scalar.copy)
-        for i in range(TILES):
+            empty_heads(tb[q], 0, q, (V, S, S, S)[q])
+        quantise_w(0, 0)
+        regroup_w(0, 1, V)
+        quantise_w(0, 1)
+        for i in range(2):
             quantise_y(0, i)
-        first_banks = multiply(0, 0)
-        for i in range(TILES // 2):
-            finish(first_banks[i], 0, 0, i)
+        sort_heads(1, 0, 0, S)
+        sort_heads(1, 0, 1, S)
+        sort_heads(1, 1, 0, V)
+        sort_heads(1, 1, 1, S)
+        for i in range(2, TILES):
+            quantise_y(0, i)
+        b00 = [multiply_tile(0, 0, i) for i in range(2)]
+        tb = [transpose_heads(1, q) for q in range(BANKS)]
+        b00 += [multiply_tile(0, 0, i) for i in range(2, 4)]
+        finish(b00[0], 0, 0, 0)
+        share_w(1, 0, 256)
+        finish(b00[1], 0, 0, 1)
+        share_w(1, 1, 256)
         quantise_w(1, 0)
         for q in range(BANKS):
-            sort_heads(1, q)
-            transpose_heads(1, q)
+            empty_heads(tb[q], 1, q, S)
         quantise_w(1, 1)
-        for i in range(TILES // 2, TILES):
-            finish(first_banks[i], 0, 0, i)
-        second_banks = multiply(0, 1)
-        for i in range(TILES):
-            quantise_y(1, i)
-        for i in range(TILES):
-            finish(second_banks[i], 0, 1, i)
-        for nh in range(N_HALVES):
-            banks = multiply(1, nh)
+        b01 = multiply(0, 1)
+        finish(b00[2], 0, 0, 2)
+        finish(b00[3], 0, 0, 3)
+        finish(b01[0], 0, 1, 0)
+        quantise_y(1, 0)
+        quantise_y(1, 1)
+        finish(b01[1], 0, 1, 1)
+        quantise_y(1, 2)
+        quantise_y(1, 3)
+        finish(b01[2], 0, 1, 2)
+        finish(b01[3], 0, 1, 3, by_scalar=True)
+        b10 = multiply(1, 0)
+        b11 = multiply(1, 1)
+        k = 0
+        for nh, banks in ((0, b10), (1, b11)):
             for i in range(TILES):
-                finish(banks[i], 1, nh, i)
+                finish(banks[i], 1, nh, i, by_scalar=(k % 3 == 1))
+                k += 1

@@ -61,7 +61,7 @@ def tile_reasoningmultiheadattention_pb_kernel(tc, h_attn, Wo, bo, out):
         y_grouped = keep.tile([P, ROUNDS, TILES * TILE_WORDS * PACK], BF16, align_bytes=64)
         y_codes = keep.tile([P, ROUNDS, TILES, TILE_WORDS], U32, align_bytes=64)
         y_scales = keep.tile([P, ROUNDS, TILES, TILE_WORDS], U8, align_bytes=64)
-        w_raw = keep.tile([P, N_HALVES, PASSES, PACK, N_HALF], BF16)
+        w_raw = keep.tile([P, PASSES, PACK, N], BF16)
         w_grouped = keep.tile([P, N_HALVES, PASSES, N_HALF * PACK], BF16, align_bytes=64)
         w_codes = keep.tile([P, PASSES, N], U32, align_bytes=64)
         w_scales = keep.tile([P, PASSES, N], U8, align_bytes=64)
@@ -73,21 +73,20 @@ def tile_reasoningmultiheadattention_pb_kernel(tc, h_attn, Wo, bo, out):
             tokens = slice(c * CHUNK, (c + 1) * CHUNK)
             nc.sync.dma_start(out=x_raw[:, r, tokens], in_=h_view[r][:, tokens])
 
-        def load_w(nh, g):
-            nc.sync.dma_start(out=w_raw[:, nh, g], in_=w_view[g][:, :, half(nh)])
+        def load_w(g, cols):
+            nc.sync.dma_start(out=w_raw[:, g, :, cols], in_=w_view[g][:, :, cols])
 
         nc.vector.memset(ones[:], 1.0)
         nc.vector.memset(bias_row[:], 0.0)
         nc.scalar.copy(out=warm[:], in_=ones[:, 0:1])
+        load_w(0, slice(0, N))
         load_x(0, 0)
         nc.sync.dma_start(out=bias_row[0:1, :], in_=bo.unsqueeze(0))
         load_x(0, 1)
-        load_w(0, 0)
-        load_w(0, 1)
+        load_w(1, half(0))
         load_x(1, 0)
         load_x(1, 1)
-        load_w(1, 0)
-        load_w(1, 1)
+        load_w(1, half(1))
         make_identity(nc, ident[:])
         nc.vector.tensor_copy(
             out=perm[:].rearrange("p (b g thi) -> p b g thi", b=BATCH, g=PASSES),
@@ -107,7 +106,9 @@ def tile_reasoningmultiheadattention_pb_kernel(tc, h_attn, Wo, bo, out):
                 out=w_grouped[:, nh, g, first * PACK : last * PACK].rearrange(
                     "p (c i t) -> p c t i", i=RUN, t=PACK
                 ),
-                in_=w_raw[:, nh, g, :, first:last].rearrange("p t (c i) -> p c t i", i=RUN),
+                in_=w_raw[:, g, :, nh * N_HALF + first : nh * N_HALF + last].rearrange(
+                    "p t (c i) -> p c t i", i=RUN
+                ),
             )
 
         def share_w(nh, g, cut):
@@ -185,63 +186,101 @@ def tile_reasoningmultiheadattention_pb_kernel(tc, h_attn, Wo, bo, out):
         def multiply(r, nh):
             return [multiply_tile(r, nh, i) for i in range(TILES)]
 
-        def finish(acc, r, nh, i, by_scalar=False):
+        def empty_v(acc, nh):
             result = results.tile([P, N_HALF], F32, name="result")
-            if by_scalar:
-                nc.scalar.copy(out=result[:], in_=acc[:])
-                nc.gpsimd.tensor_tensor(out=result[:], in0=result[:], in1=bias[:, half(nh)], op=ADD)
-            else:
-                nc.vector.tensor_tensor(out=result[:], in0=acc[:], in1=bias[:, half(nh)], op=ADD)
+            nc.vector.tensor_tensor(out=result[:], in0=acc[:], in1=bias[:, half(nh)], op=ADD)
+            return result
+
+        def empty_s(acc, nh):
+            result = results.tile([P, N_HALF], F32, name="result")
+            nc.scalar.copy(out=result[:], in_=acc[:])
+            nc.gpsimd.tensor_tensor(out=result[:], in0=result[:], in1=bias[:, half(nh)], op=ADD)
+            return result
+
+        def store(result, r, nh, i):
             row = i * TOKENS + r * P
             nc.sync.dma_start(out=out_rows[row : row + P, half(nh)], in_=result[:])
 
+        def finish(acc, r, nh, i):
+            store(empty_v(acc, nh), r, nh, i)
+
+        def finish_group(banks, r, nh, scalar_tiles, between=()):
+            late = None
+            steps = list(between)
+            for i in range(TILES):
+                if i in scalar_tiles:
+                    late = (empty_s(banks[i], nh), r, nh, i)
+                else:
+                    store(empty_v(banks[i], nh), r, nh, i)
+                    if late is not None:
+                        store(*late)
+                        late = None
+                if steps:
+                    steps.pop(0)()
+            if late is not None:
+                store(*late)
+
         V, S = nc.vector.tensor_copy, nc.scalar.copy
+        regroup_w(0, 0, V)
+        regroup_w(1, 0, S)
+        quantise_w(0, 0)
         sort_heads(0, 0, 0, V)
         sort_heads(0, 0, 1, V)
-        spread_bias()
         sort_heads(0, 1, 0, S)
         sort_heads(0, 1, 1, V)
+        spread_bias()
+        quantise_w(1, 0)
+        warm_up(x_raw[:, 0, CHUNK], 2)
         tb = [transpose_heads(0, q) for q in range(BANKS)]
-        share_w(0, 0, 256)
         for q in range(BANKS):
-            empty_heads(tb[q], 0, q, (V, S, S, S)[q])
-        quantise_w(0, 0)
+            empty_heads(tb[q], 0, q, S)
         regroup_w(0, 1, V)
+        warm_up(x_raw[:, 1, 0], 2)
+        sort_heads(1, 0, 1, V)
         quantise_w(0, 1)
-        for i in range(2):
-            quantise_y(0, i)
+        quantise_y(0, 0)
+        quantise_y(0, 1)
         sort_heads(1, 0, 0, S)
-        sort_heads(1, 0, 1, S)
         sort_heads(1, 1, 0, V)
         sort_heads(1, 1, 1, S)
-        for i in range(2, TILES):
-            quantise_y(0, i)
-        b00 = [multiply_tile(0, 0, i) for i in range(2)]
+        quantise_y(0, 2)
+        quantise_y(0, 3)
+        b00 = [multiply_tile(0, 0, i) for i in range(4)]
         tb = [transpose_heads(1, q) for q in range(BANKS)]
-        b00 += [multiply_tile(0, 0, i) for i in range(2, 4)]
+        b00 += [multiply_tile(0, 0, i) for i in range(4, TILES)]
+        share_w(1, 1, 320)
         finish(b00[0], 0, 0, 0)
-        share_w(1, 0, 256)
-        finish(b00[1], 0, 0, 1)
-        share_w(1, 1, 256)
-        quantise_w(1, 0)
-        for q in range(BANKS):
-            empty_heads(tb[q], 1, q, S)
+        t1 = empty_s(b00[1], 0)
         quantise_w(1, 1)
         b01 = multiply(0, 1)
         finish(b00[2], 0, 0, 2)
-        finish(b00[3], 0, 0, 3)
+        store(t1, 0, 0, 1)
+        t3 = empty_s(b00[3], 0)
+        empty_heads(tb[0], 1, 0, V)
+        empty_heads(tb[1], 1, 1, S)
+        empty_heads(tb[2], 1, 2, S)
+        empty_heads(tb[3], 1, 3, S)
         finish(b01[0], 0, 1, 0)
+        store(t3, 0, 0, 3)
         quantise_y(1, 0)
-        quantise_y(1, 1)
+        b1 = [[multiply_tile(1, nh, 0) for nh in range(N_HALVES)]]
         finish(b01[1], 0, 1, 1)
+        t2 = empty_s(b01[2], 1)
+        quantise_y(1, 1)
+        b1.append([multiply_tile(1, nh, 1) for nh in range(N_HALVES)])
+        finish(b01[3], 0, 1, 3)
+        store(t2, 0, 1, 2)
         quantise_y(1, 2)
+        b1.append([multiply_tile(1, nh, 2) for nh in range(N_HALVES)])
+        finish(b1[0][0], 1, 0, 0)
         quantise_y(1, 3)
-        finish(b01[2], 0, 1, 2)
-        finish(b01[3], 0, 1, 3, by_scalar=True)
-        b10 = multiply(1, 0)
-        b11 = multiply(1, 1)
-        k = 0
-        for nh, banks in ((0, b10), (1, b11)):
-            for i in range(TILES):
-                finish(banks[i], 1, nh, i, by_scalar=(k % 3 == 1))
-                k += 1
+        b1.append([multiply_tile(1, nh, 3) for nh in range(N_HALVES)])
+        late = empty_s(b1[0][1], 1)
+        finish(b1[1][0], 1, 0, 1)
+        store(late, 1, 1, 0)
+        finish(b1[1][1], 1, 1, 1)
+        late = empty_s(b1[2][0], 0)
+        finish(b1[2][1], 1, 1, 2)
+        store(late, 1, 0, 2)
+        finish(b1[3][0], 1, 0, 3)
+        finish(b1[3][1], 1, 1, 3)

@@ -61,7 +61,8 @@ def tile_reasoningmultiheadattention_pb_kernel(tc, h_attn, Wo, bo, out):
         y_grouped = keep.tile([P, ROUNDS, TILES * TILE_WORDS * PACK], BF16, align_bytes=64)
         y_codes = keep.tile([P, ROUNDS, TILES, TILE_WORDS], U32, align_bytes=64)
         y_scales = keep.tile([P, ROUNDS, TILES, TILE_WORDS], U8, align_bytes=64)
-        w_raw = keep.tile([P, PASSES, PACK, N], BF16)
+        w_whole = keep.tile([P, PACK, N], BF16)
+        w_halves = [keep.tile([P, PACK, N_HALF], BF16, name="w_half", bufs=2) for nh in range(N_HALVES)]
         w_grouped = keep.tile([P, N_HALVES, PASSES, N_HALF * PACK], BF16, align_bytes=64)
         w_codes = keep.tile([P, PASSES, N], U32, align_bytes=64)
         w_scales = keep.tile([P, PASSES, N], U8, align_bytes=64)
@@ -73,20 +74,26 @@ def tile_reasoningmultiheadattention_pb_kernel(tc, h_attn, Wo, bo, out):
             tokens = slice(c * CHUNK, (c + 1) * CHUNK)
             nc.sync.dma_start(out=x_raw[:, r, tokens], in_=h_view[r][:, tokens])
 
-        def load_w(g, cols):
-            nc.sync.dma_start(out=w_raw[:, g, :, cols], in_=w_view[g][:, :, cols])
+        def load_w_whole():
+            nc.sync.dma_start(out=w_whole[:], in_=w_view[0])
+
+        def load_w_half(nh):
+            nc.sync.dma_start(out=w_halves[nh][:], in_=w_view[1][:, :, half(nh)])
+
+        def w_rows(nh, g):
+            return w_halves[nh] if g else w_whole[:, :, half(nh)]
 
         nc.vector.memset(ones[:], 1.0)
         nc.vector.memset(bias_row[:], 0.0)
         nc.scalar.copy(out=warm[:], in_=ones[:, 0:1])
-        load_w(0, slice(0, N))
+        load_w_whole()
         load_x(0, 0)
         nc.sync.dma_start(out=bias_row[0:1, :], in_=bo.unsqueeze(0))
         load_x(0, 1)
-        load_w(1, half(0))
+        load_w_half(0)
         load_x(1, 0)
         load_x(1, 1)
-        load_w(1, half(1))
+        load_w_half(1)
         make_identity(nc, ident[:])
         nc.vector.tensor_copy(
             out=perm[:].rearrange("p (b g thi) -> p b g thi", b=BATCH, g=PASSES),
@@ -106,9 +113,7 @@ def tile_reasoningmultiheadattention_pb_kernel(tc, h_attn, Wo, bo, out):
                 out=w_grouped[:, nh, g, first * PACK : last * PACK].rearrange(
                     "p (c i t) -> p c t i", i=RUN, t=PACK
                 ),
-                in_=w_raw[:, g, :, nh * N_HALF + first : nh * N_HALF + last].rearrange(
-                    "p t (c i) -> p c t i", i=RUN
-                ),
+                in_=w_rows(nh, g)[:, :, first:last].rearrange("p t (c i) -> p c t i", i=RUN),
             )
 
         def share_w(nh, g, cut):
@@ -248,20 +253,20 @@ def tile_reasoningmultiheadattention_pb_kernel(tc, h_attn, Wo, bo, out):
         b00 = [multiply_tile(0, 0, i) for i in range(4)]
         tb = [transpose_heads(1, q) for q in range(BANKS)]
         b00 += [multiply_tile(0, 0, i) for i in range(4, TILES)]
-        share_w(1, 1, 320)
+        regroup_w(1, 1, V, last=256)
+        regroup_w(1, 1, S, first=256)
         finish(b00[0], 0, 0, 0)
         t1 = empty_s(b00[1], 0)
         quantise_w(1, 1)
         b01 = multiply(0, 1)
         finish(b00[2], 0, 0, 2)
         store(t1, 0, 0, 1)
-        t3 = empty_s(b00[3], 0)
-        empty_heads(tb[0], 1, 0, V)
+        finish(b00[3], 0, 0, 3)
+        empty_heads(tb[0], 1, 0, S)
         empty_heads(tb[1], 1, 1, S)
         empty_heads(tb[2], 1, 2, S)
         empty_heads(tb[3], 1, 3, S)
         finish(b01[0], 0, 1, 0)
-        store(t3, 0, 0, 3)
         quantise_y(1, 0)
         b1 = [[multiply_tile(1, nh, 0) for nh in range(N_HALVES)]]
         finish(b01[1], 0, 1, 1)
@@ -278,9 +283,10 @@ def tile_reasoningmultiheadattention_pb_kernel(tc, h_attn, Wo, bo, out):
         late = empty_s(b1[0][1], 1)
         finish(b1[1][0], 1, 0, 1)
         store(late, 1, 1, 0)
-        finish(b1[1][1], 1, 1, 1)
-        late = empty_s(b1[2][0], 0)
-        finish(b1[2][1], 1, 1, 2)
-        store(late, 1, 0, 2)
+        late = empty_s(b1[1][1], 1)
+        finish(b1[2][0], 1, 0, 2)
+        store(late, 1, 1, 1)
+        late = empty_s(b1[2][1], 1)
         finish(b1[3][0], 1, 0, 3)
+        store(late, 1, 1, 2)
         finish(b1[3][1], 1, 1, 3)

@@ -246,46 +246,41 @@ def tile_reasoningmultiheadattention_pb_kernel(tc, h_attn, Wo, bo, out):
         quantise_y(0, 0)
         quantise_y(0, 1)
         sort_heads(1, 0, 0, S)
-        sort_heads(1, 1, 0, V)
+        sort_heads(1, 1, 0, S)
         sort_heads(1, 1, 1, S)
         quantise_y(0, 2)
         quantise_y(0, 3)
-        b00 = [multiply_tile(0, 0, i) for i in range(4)]
+        b00 = multiply(0, 0)
         tb = [transpose_heads(1, q) for q in range(BANKS)]
-        b00 += [multiply_tile(0, 0, i) for i in range(4, TILES)]
+        finish(b00[0], 0, 0, 0)
         regroup_w(1, 1, V, last=256)
         regroup_w(1, 1, S, first=256)
-        finish(b00[0], 0, 0, 0)
-        t1 = empty_s(b00[1], 0)
+        finish(b00[1], 0, 0, 1)
+        for q in range(BANKS):
+            empty_heads(tb[q], 1, q, S)
         quantise_w(1, 1)
         b01 = multiply(0, 1)
+        b1 = []
         finish(b00[2], 0, 0, 2)
-        store(t1, 0, 0, 1)
         finish(b00[3], 0, 0, 3)
-        empty_heads(tb[0], 1, 0, S)
-        empty_heads(tb[1], 1, 1, S)
-        empty_heads(tb[2], 1, 2, S)
-        empty_heads(tb[3], 1, 3, S)
         finish(b01[0], 0, 1, 0)
-        quantise_y(1, 0)
-        b1 = [[multiply_tile(1, nh, 0) for nh in range(N_HALVES)]]
         finish(b01[1], 0, 1, 1)
-        t2 = empty_s(b01[2], 1)
+        quantise_y(1, 0)
+        b1.append([multiply_tile(1, nh, 0) for nh in range(N_HALVES)])
         quantise_y(1, 1)
         b1.append([multiply_tile(1, nh, 1) for nh in range(N_HALVES)])
-        finish(b01[3], 0, 1, 3)
-        store(t2, 0, 1, 2)
         quantise_y(1, 2)
         b1.append([multiply_tile(1, nh, 2) for nh in range(N_HALVES)])
-        finish(b1[0][0], 1, 0, 0)
         quantise_y(1, 3)
         b1.append([multiply_tile(1, nh, 3) for nh in range(N_HALVES)])
-        late = empty_s(b1[0][1], 1)
-        finish(b1[1][0], 1, 0, 1)
-        store(late, 1, 1, 0)
-        late = empty_s(b1[1][1], 1)
+        finish(b01[2], 0, 1, 2)
+        finish(b01[3], 0, 1, 3)
+        finish(b1[0][0], 1, 0, 0)
+        finish(b1[0][1], 1, 1, 0)
+        late = empty_s(b1[1][0], 0)
+        finish(b1[1][1], 1, 1, 1)
+        store(late, 1, 0, 1)
         finish(b1[2][0], 1, 0, 2)
-        store(late, 1, 1, 1)
         late = empty_s(b1[2][1], 1)
         finish(b1[3][0], 1, 0, 3)
         store(late, 1, 1, 2)

@@ -40,7 +40,8 @@ def tile_reasoningmultiheadattention_pb_kernel(tc, h_attn, Wo, bo, out):
     with ExitStack() as stack:
         const = stack.enter_context(tc.tile_pool(name="const", bufs=1))
         keep = stack.enter_context(tc.tile_pool(name="keep", bufs=1))
-        results = stack.enter_context(tc.tile_pool(name="results", bufs=16))
+        results = stack.enter_context(tc.tile_pool(name="results", bufs=12))
+        wide = stack.enter_context(tc.tile_pool(name="wide", bufs=4))
         psum = stack.enter_context(tc.psum_pool(name="psum", bufs=8))
         stack.enter_context(tc.manual_schedule())
 
@@ -209,6 +210,22 @@ def tile_reasoningmultiheadattention_pb_kernel(tc, h_attn, Wo, bo, out):
         def finish(acc, r, nh, i):
             store(empty_v(acc, nh), r, nh, i)
 
+        def new_rows():
+            return wide.tile([P, N], F32, name="rows")
+
+        def rows_v(rows, acc, nh):
+            nc.vector.tensor_tensor(out=rows[:, half(nh)], in0=acc[:], in1=bias[:, half(nh)], op=ADD)
+
+        def rows_s(rows, acc, nh):
+            nc.scalar.copy(out=rows[:, half(nh)], in_=acc[:])
+            nc.gpsimd.tensor_tensor(
+                out=rows[:, half(nh)], in0=rows[:, half(nh)], in1=bias[:, half(nh)], op=ADD
+            )
+
+        def store_rows(rows, r, i):
+            row = i * TOKENS + r * P
+            nc.sync.dma_start(out=out_rows[row : row + P, :], in_=rows[:])
+
         def finish_group(banks, r, nh, scalar_tiles, between=()):
             late = None
             steps = list(between)
@@ -228,11 +245,12 @@ def tile_reasoningmultiheadattention_pb_kernel(tc, h_attn, Wo, bo, out):
         V, S = nc.vector.tensor_copy, nc.scalar.copy
         regroup_w(0, 0, V)
         regroup_w(1, 0, S)
-        quantise_w(0, 0)
         sort_heads(0, 0, 0, V)
         sort_heads(0, 0, 1, V)
-        sort_heads(0, 1, 0, S)
+        quantise_w(0, 0)
         sort_heads(0, 1, 1, V)
+        sort_heads(0, 1, 0, V, last=2)
+        sort_heads(0, 1, 0, S, first=2)
         spread_bias()
         quantise_w(1, 0)
         warm_up(x_raw[:, 0, CHUNK], 2)
@@ -277,11 +295,13 @@ def tile_reasoningmultiheadattention_pb_kernel(tc, h_attn, Wo, bo, out):
         finish(b01[3], 0, 1, 3)
         finish(b1[0][0], 1, 0, 0)
         finish(b1[0][1], 1, 1, 0)
-        late = empty_s(b1[1][0], 0)
-        finish(b1[1][1], 1, 1, 1)
-        store(late, 1, 0, 1)
-        finish(b1[2][0], 1, 0, 2)
-        late = empty_s(b1[2][1], 1)
+        rows1 = new_rows()
+        rows_s(rows1, b1[1][0], 0)
+        rows_v(rows1, b1[1][1], 1)
+        rows2 = new_rows()
+        rows_v(rows2, b1[2][0], 0)
+        store_rows(rows1, 1, 1)
+        rows_s(rows2, b1[2][1], 1)
         finish(b1[3][0], 1, 0, 3)
-        store(late, 1, 1, 2)
         finish(b1[3][1], 1, 1, 3)
+        store_rows(rows2, 1, 2)

@@ -9,6 +9,7 @@ U32 = mybir.dt.uint32
 U8 = mybir.dt.uint8
 FP8X4 = mybir.dt.float8_e4m3fn_x4
 ADD = mybir.AluOpType.add
+MULT = mybir.AluOpType.mult
 
 P = 128
 BATCH, TOKENS, HEADS, DH = 4, 256, 16, 64
@@ -108,6 +109,11 @@ def tile_reasoningmultiheadattention_pb_kernel(tc, h_attn, Wo, bo, out):
                     out=spread[:, half(nh)], lhsT=ones[:], rhs=bias_row[:, half(nh)], start=True, stop=True
                 )
             nc.scalar.copy(out=bias[:], in_=spread[:])
+
+        def gpsimd_copy(out, in_):
+            nc.gpsimd.tensor_scalar(
+                out=out, in0=in_, scalar1=1.0, scalar2=0.0, op0=MULT, op1=ADD
+            )
 
         def regroup_w(nh, g, copy, first=0, last=N_HALF):
             copy(
@@ -268,18 +274,19 @@ def tile_reasoningmultiheadattention_pb_kernel(tc, h_attn, Wo, bo, out):
         sort_heads(1, 1, 1, S)
         quantise_y(0, 2)
         quantise_y(0, 3)
-        b00 = multiply(0, 0)
+        b00 = [multiply_tile(0, 0, i) for i in range(3)]
         tb = [transpose_heads(1, q) for q in range(BANKS)]
+        b00 += [multiply_tile(0, 0, i) for i in range(3, TILES)]
         finish(b00[0], 0, 0, 0)
-        regroup_w(1, 1, V, last=256)
+        regroup_w(1, 1, gpsimd_copy, last=256)
         regroup_w(1, 1, S, first=256)
         finish(b00[1], 0, 0, 1)
         for q in range(BANKS):
             empty_heads(tb[q], 1, q, S)
+        finish(b00[2], 0, 0, 2)
         quantise_w(1, 1)
         b01 = multiply(0, 1)
         b1 = []
-        finish(b00[2], 0, 0, 2)
         finish(b00[3], 0, 0, 3)
         finish(b01[0], 0, 1, 0)
         finish(b01[1], 0, 1, 1)

@@ -72,8 +72,13 @@ def tile_reasoningmultiheadattention_pb_kernel(tc, h_attn, Wo, bo, out):
         def half(nh):
             return slice(nh * N_HALF, (nh + 1) * N_HALF)
 
+        def chunk(c):
+            if c < 2:
+                return slice(c * CHUNK, (c + 1) * CHUNK)
+            return slice(2 * c, 2 * c + 2)
+
         def load_x(r, c):
-            tokens = slice(c * CHUNK, (c + 1) * CHUNK)
+            tokens = chunk(c)
             nc.sync.dma_start(out=x_raw[:, r, tokens], in_=h_view[r][:, tokens])
 
         def load_w_whole():
@@ -91,7 +96,8 @@ def tile_reasoningmultiheadattention_pb_kernel(tc, h_attn, Wo, bo, out):
         load_w_whole()
         load_x(0, 0)
         nc.sync.dma_start(out=bias_row[0:1, :], in_=bo.unsqueeze(0))
-        load_x(0, 1)
+        load_x(0, 2)
+        load_x(0, 3)
         load_w_half(0)
         load_x(1, 0)
         load_x(1, 1)
@@ -140,7 +146,7 @@ def tile_reasoningmultiheadattention_pb_kernel(tc, h_attn, Wo, bo, out):
             )
 
         def sort_heads(r, c, u, copy, first=0, last=ROUND_HEADS):
-            tokens = slice(c * CHUNK, (c + 1) * CHUNK)
+            tokens = chunk(c)
             copy(
                 out=by_head[:, r, u].rearrange("p (h j w) -> p h j w", h=ROUND_HEADS, j=JL)[
                     :, first:last, tokens
@@ -253,10 +259,12 @@ def tile_reasoningmultiheadattention_pb_kernel(tc, h_attn, Wo, bo, out):
         regroup_w(1, 0, S)
         sort_heads(0, 0, 0, V)
         sort_heads(0, 0, 1, V)
+        sort_heads(0, 2, 1, V)
+        sort_heads(0, 2, 0, S)
+        sort_heads(0, 3, 1, V)
+        sort_heads(0, 3, 0, V, last=2)
+        sort_heads(0, 3, 0, S, first=2)
         quantise_w(0, 0)
-        sort_heads(0, 1, 1, V)
-        sort_heads(0, 1, 0, V, last=2)
-        sort_heads(0, 1, 0, S, first=2)
         spread_bias()
         quantise_w(1, 0)
         warm_up(x_raw[:, 0, CHUNK], 2)

from contextlib import ExitStack

from concourse import mybir
from concourse.masks import make_identity

BF16 = mybir.dt.bfloat16
F32 = mybir.dt.float32
U32 = mybir.dt.uint32
U8 = mybir.dt.uint8
FP8X4 = mybir.dt.float8_e4m3fn_x4
ADD = mybir.AluOpType.add
MULT = mybir.AluOpType.mult

P = 128
BATCH, TOKENS, HEADS, DH = 4, 256, 16, 64
ROW_TOKENS = 16
THI = TOKENS // ROW_TOKENS
K = ROW_TOKENS * DH
N = 1024
PACK = 4
PASSES = K // (PACK * P)
N_HALF = 512
N_HALVES = N // N_HALF
ROUNDS = 2
ROUND_HEADS = HEADS // ROUNDS
JL = 8
WORDS = DH // 4
BANK_HEADS = 2
BANKS = ROUND_HEADS // BANK_HEADS
CHUNKS = 2
CHUNK = JL // CHUNKS
TILES = BATCH
TILE_WORDS = PASSES * P
RUN = 4

FLOPS = 2 * BATCH * TOKENS * K * N


def tile_reasoningmultiheadattention_pb_kernel(tc, h_attn, Wo, bo, out):
    nc = tc.nc
    with ExitStack() as stack:
        const = stack.enter_context(tc.tile_pool(name="const", bufs=1))
        keep = stack.enter_context(tc.tile_pool(name="keep", bufs=1))
        results = stack.enter_context(tc.tile_pool(name="results", bufs=12))
        wide = stack.enter_context(tc.tile_pool(name="wide", bufs=4))
        psum = stack.enter_context(tc.psum_pool(name="psum", bufs=8))
        stack.enter_context(tc.manual_schedule())

        h_view = h_attn.rearrange(
            "b (t8 j) (r h) d -> r (b t8) j (h d)", j=JL, r=ROUNDS
        )
        w_view = Wo.rearrange("(g p t) n -> g p t n", g=PASSES, t=PACK)
        out_rows = out.flatten_outer_dims()

        bias_row = const.tile([P, N], BF16)
        ones = const.tile([P, P], BF16)
        warm = const.tile([P, 1], BF16)
        ident = const.tile([P, P], F32)
        perm = const.tile([P, P], F32)
        bias = const.tile([P, N], BF16)
        x_raw = keep.tile([P, ROUNDS, JL, ROUND_HEADS * DH], BF16)
        by_head = keep.tile([P, ROUNDS, 2, ROUND_HEADS * P], F32)
        y_grouped = keep.tile([P, ROUNDS, TILES * TILE_WORDS * PACK], BF16, align_bytes=64)
        y_codes = keep.tile([P, ROUNDS, TILES, TILE_WORDS], U32, align_bytes=64)
        y_scales = keep.tile([P, ROUNDS, TILES, TILE_WORDS], U8, align_bytes=64)
        w_whole = keep.tile([P, PACK, N], BF16)
        w_halves = [keep.tile([P, PACK, N_HALF], BF16, name="w_half", bufs=2) for nh in range(N_HALVES)]
        w_grouped = keep.tile([P, N_HALVES, PASSES, N_HALF * PACK], BF16, align_bytes=64)
        w_codes = keep.tile([P, PASSES, N], U32, align_bytes=64)
        w_scales = keep.tile([P, PASSES, N], U8, align_bytes=64)

        def half(nh):
            return slice(nh * N_HALF, (nh + 1) * N_HALF)

        def chunk(c):
            if c < 2:
                return slice(c * CHUNK, (c + 1) * CHUNK)
            return slice(2 * c, 2 * c + 2)

        def load_x(r, c):
            tokens = chunk(c)
            nc.sync.dma_start(out=x_raw[:, r, tokens], in_=h_view[r][:, tokens])

        def load_w_whole():
            nc.sync.dma_start(out=w_whole[:], in_=w_view[0])

        def load_w_half(nh):
            nc.sync.dma_start(out=w_halves[nh][:], in_=w_view[1][:, :, half(nh)])

        def w_rows(nh, g):
            return w_halves[nh] if g else w_whole[:, :, half(nh)]

        nc.vector.memset(ones[:], 1.0)
        nc.vector.memset(bias_row[:], 0.0)
        nc.scalar.copy(out=warm[:], in_=ones[:, 0:1])
        load_w_whole()
        load_x(0, 0)
        nc.sync.dma_start(out=bias_row[0:1, :], in_=bo.unsqueeze(0))
        load_x(0, 2)
        load_x(0, 3)
        load_w_half(0)
        load_x(1, 0)
        load_x(1, 1)
        load_w_half(1)
        make_identity(nc, ident[:])
        nc.vector.tensor_copy(
            out=perm[:].rearrange("p (b g thi) -> p b g thi", b=BATCH, g=PASSES),
            in_=ident[:].rearrange("p (b thi g) -> p b g thi", b=BATCH, g=PASSES),
        )

        def spread_bias():
            spread = psum.tile([P, N], BF16, name="bank")
            for nh in range(N_HALVES):
                nc.tensor.matmul(
                    out=spread[:, half(nh)], lhsT=ones[:], rhs=bias_row[:, half(nh)], start=True, stop=True
                )
            nc.scalar.copy(out=bias[:], in_=spread[:])

        def gpsimd_copy(out, in_):
            nc.gpsimd.tensor_scalar(
                out=out, in0=in_, scalar1=1.0, scalar2=0.0, op0=MULT, op1=ADD
            )

        def regroup_w(nh, g, copy, first=0, last=N_HALF):
            copy(
                out=w_grouped[:, nh, g, first * PACK : last * PACK].rearrange(
                    "p (c i t) -> p c t i", i=RUN, t=PACK
                ),
                in_=w_rows(nh, g)[:, :, first:last].rearrange("p t (c i) -> p c t i", i=RUN),
            )

        def share_w(nh, g, cut):
            regroup_w(nh, g, nc.vector.tensor_copy, last=cut)
            regroup_w(nh, g, nc.scalar.copy, first=cut)

        def warm_up(rhs, count):
            bank = psum.tile([P, N_HALF], F32, name="bank")
            for k in range(count):
                nc.tensor.matmul(out=bank[:], lhsT=ones[:], rhs=rhs, start=True, stop=True)

        def quantise_w(nh, g):
            nc.vector.quantize_mx(
                out=w_codes[:, g, half(nh)].bitcast(FP8X4),
                scales=w_scales[:, g, half(nh)],
                in_=w_grouped[:, nh, g],
            )

        def sort_heads(r, c, u, copy, first=0, last=ROUND_HEADS):
            tokens = chunk(c)
            copy(
                out=by_head[:, r, u].rearrange("p (h j w) -> p h j w", h=ROUND_HEADS, j=JL)[
                    :, first:last, tokens
                ],
                in_=x_raw[:, r].rearrange("p j hd -> p (j hd)").bitcast(F32).rearrange(
                    "p (j h w u) -> p u h j w", j=JL, h=ROUND_HEADS, u=2
                )[:, u, first:last, tokens],
            )

        def transpose_heads(r, q):
            bank = psum.tile([P, N_HALF], F32, name="bank")
            for h in range(BANK_HEADS):
                for u in range(2):
                    first = (BANK_HEADS * q + h) * P
                    nc.tensor.transpose(
                        bank[:].rearrange(
                            "p (bg h u thi) -> p bg h u thi", h=BANK_HEADS, u=2, thi=THI
                        )[:, :, h, u],
                        by_head[:, r, u, first : first + P],
                        perm[:],
                    )
            return bank

        def empty_heads(bank, r, q, copy):
            copy(
                out=y_grouped[:, r].bitcast(F32).rearrange(
                    "p (bg h thi u) -> p bg h thi u", h=ROUND_HEADS, thi=THI, u=2
                )[:, :, BANK_HEADS * q : BANK_HEADS * (q + 1)],
                in_=bank[:].rearrange(
                    "p (bg h u thi) -> p bg h thi u", h=BANK_HEADS, u=2, thi=THI
                ),
            )

        def quantise_y(r, i):
            nc.vector.quantize_mx(
                out=y_codes[:, r, i].bitcast(FP8X4),
                scales=y_scales[:, r, i],
                in_=y_grouped[:, r, i * TILE_WORDS * PACK : (i + 1) * TILE_WORDS * PACK],
            )

        def multiply_tile(r, nh, i):
            acc = psum.tile([P, N_HALF], F32, name="bank")
            for g in range(PASSES):
                nc.tensor.matmul_mx(
                    out=acc[:],
                    lhsT=y_codes[:, r, i, g * P : (g + 1) * P].bitcast(FP8X4),
                    lhsT_scale=y_scales[:, r, i, g * P : (g + 1) * P],
                    rhs=w_codes[:, g, half(nh)].bitcast(FP8X4),
                    rhs_scale=w_scales[:, g, half(nh)],
                    start=(g == 0),
                    stop=(g == PASSES - 1),
                )
            return acc

        def multiply(r, nh):
            return [multiply_tile(r, nh, i) for i in range(TILES)]

        def empty_v(acc, nh):
            result = results.tile([P, N_HALF], F32, name="result")
            nc.vector.tensor_tensor(out=result[:], in0=acc[:], in1=bias[:, half(nh)], op=ADD)
            return result

        def empty_s(acc, nh):
            result = results.tile([P, N_HALF], F32, name="result")
            nc.scalar.copy(out=result[:], in_=acc[:])
            nc.gpsimd.tensor_tensor(out=result[:], in0=result[:], in1=bias[:, half(nh)], op=ADD)
            return result

        def store(result, r, nh, i):
            row = i * TOKENS + r * P
            nc.sync.dma_start(out=out_rows[row : row + P, half(nh)], in_=result[:])

        def finish(acc, r, nh, i):
            store(empty_v(acc, nh), r, nh, i)

        def new_rows():
            return wide.tile([P, N], F32, name="rows")

        def rows_v(rows, acc, nh):
            nc.vector.tensor_tensor(out=rows[:, half(nh)], in0=acc[:], in1=bias[:, half(nh)], op=ADD)

        def rows_s(rows, acc, nh):
            nc.scalar.copy(out=rows[:, half(nh)], in_=acc[:])
            nc.gpsimd.tensor_tensor(
                out=rows[:, half(nh)], in0=rows[:, half(nh)], in1=bias[:, half(nh)], op=ADD
            )

        def store_rows(rows, r, i):
            row = i * TOKENS + r * P
            nc.sync.dma_start(out=out_rows[row : row + P, :], in_=rows[:])

        def finish_group(banks, r, nh, scalar_tiles, between=()):
            late = None
            steps = list(between)
            for i in range(TILES):
                if i in scalar_tiles:
                    late = (empty_s(banks[i], nh), r, nh, i)
                else:
                    store(empty_v(banks[i], nh), r, nh, i)
                    if late is not None:
                        store(*late)
                        late = None
                if steps:
                    steps.pop(0)()
            if late is not None:
                store(*late)

        V, S = nc.vector.tensor_copy, nc.scalar.copy
        regroup_w(0, 0, V)
        regroup_w(1, 0, S)
        sort_heads(0, 0, 0, V)
        sort_heads(0, 0, 1, V)
        sort_heads(0, 2, 1, V)
        sort_heads(0, 2, 0, S)
        sort_heads(0, 3, 1, V)
        sort_heads(0, 3, 0, V, last=2)
        sort_heads(0, 3, 0, S, first=2)
        quantise_w(0, 0)
        spread_bias()
        quantise_w(1, 0)
        warm_up(x_raw[:, 0, CHUNK], 2)
        tb = [transpose_heads(0, q) for q in range(BANKS)]
        for q in range(BANKS):
            empty_heads(tb[q], 0, q, S)
        regroup_w(0, 1, V)
        warm_up(x_raw[:, 1, 0], 2)
        sort_heads(1, 0, 1, V)
        quantise_w(0, 1)
        quantise_y(0, 0)
        quantise_y(0, 1)
        sort_heads(1, 0, 0, S)
        sort_heads(1, 1, 0, S)
        sort_heads(1, 1, 1, S)
        quantise_y(0, 2)
        quantise_y(0, 3)
        b00 = [multiply_tile(0, 0, i) for i in range(3)]
        tb = [transpose_heads(1, q) for q in range(BANKS)]
        b00 += [multiply_tile(0, 0, i) for i in range(3, TILES)]
        finish(b00[0], 0, 0, 0)
        regroup_w(1, 1, gpsimd_copy, last=256)
        regroup_w(1, 1, S, first=256)
        finish(b00[1], 0, 0, 1)
        for q in range(BANKS):
            empty_heads(tb[q], 1, q, S)
        finish(b00[2], 0, 0, 2)
        quantise_w(1, 1)
        b01 = multiply(0, 1)
        b1 = []
        finish(b00[3], 0, 0, 3)
        finish(b01[0], 0, 1, 0)
        finish(b01[1], 0, 1, 1)
        quantise_y(1, 0)
        b1.append([multiply_tile(1, nh, 0) for nh in range(N_HALVES)])
        quantise_y(1, 1)
        b1.append([multiply_tile(1, nh, 1) for nh in range(N_HALVES)])
        quantise_y(1, 2)
        b1.append([multiply_tile(1, nh, 2) for nh in range(N_HALVES)])
        quantise_y(1, 3)
        b1.append([multiply_tile(1, nh, 3) for nh in range(N_HALVES)])
        finish(b01[2], 0, 1, 2)
        finish(b01[3], 0, 1, 3)
        finish(b1[0][0], 1, 0, 0)
        finish(b1[0][1], 1, 1, 0)
        rows1 = new_rows()
        rows_s(rows1, b1[1][0], 0)
        rows_v(rows1, b1[1][1], 1)
        rows2 = new_rows()
        rows_v(rows2, b1[2][0], 0)
        store_rows(rows1, 1, 1)
        rows_s(rows2, b1[2][1], 1)
        finish(b1[3][0], 1, 0, 3)
        finish(b1[3][1], 1, 1, 3)
        store_rows(rows2, 1, 2)
